import numpy as np
import ml_dtypes


def mxq(x, axis, fmt="e4m3"):
    dtype, down = {"e4m3": (ml_dtypes.float8_e4m3fn, 7), "e5m2": (ml_dtypes.float8_e5m2, 14)}[fmt]
    v = np.moveaxis(np.asarray(x, np.float32).astype(ml_dtypes.bfloat16).astype(np.float64), axis, -1)
    blocks = v.reshape(v.shape[:-1] + (-1, 32))
    amax = np.abs(blocks).max(-1, keepdims=True)
    byte = np.maximum(np.where(amax > 0, np.frexp(amax)[1] - 1 + 127, 0) - down, 1)
    scale = np.exp2(byte - 127.0)
    codes = (blocks / scale).astype(np.float32).astype(dtype).astype(np.float64)
    return np.moveaxis((codes * scale).reshape(v.shape), -1, axis)


WIDE = False


def mx_kscale(k):
    if not WIDE:
        return np.ones(k)
    levels = np.array([10, -10, 5, -5, 0])
    a = np.random.permutation(np.resize(levels, k // 512 * 4)).reshape(k // 512, 4)
    idx = np.arange(k)
    return np.exp2(a[idx // 512, idx % 128 // 32])


BF16 = ml_dtypes.bfloat16


def bf(x):
    return np.asarray(x, np.float32).astype(BF16)


def f64(x):
    return np.asarray(x).astype(np.float64)


B, S, H, R, K, RK = 4, 256, 2048, 512, 128, 512
ALPHA = 0.35


def setup_inputs():
    t = mx_kscale(RK)
    e = np.exp(1.7 * np.random.standard_normal((B, S, K)) - 5.0)
    return {
        "hidden_states": bf(np.random.standard_normal((B, S, H)) + 0.5),
        "Wd": bf(np.random.standard_normal((RK, H)) * 2.0 / np.sqrt(H) * t[:, None]),
        "Wu": bf(np.random.standard_normal((H, RK)) * 3.0 / np.sqrt(RK) / t),
        "mode_probs": bf(e / (1.0 + e.sum(-1, keepdims=True))),
        "gate": bf(np.tanh(np.random.standard_normal((K, RK)))),
    }


def reference(hidden_states, Wd, Wu, mode_probs, gate):
    x = f64(hidden_states)
    low_rank = mxq(x, 2, "e4m3") @ mxq(f64(Wd), 1, "e4m3").T
    weighted_gate = f64(mode_probs) @ f64(gate)
    h = low_rank * weighted_gate
    delta = ALPHA * (mxq(h, 2, "e4m3") @ mxq(f64(Wu), 1, "e4m3").T)
    return x + delta

@@ -1,0 +1,243 @@
+from contextlib import ExitStack
+
+import concourse.mybir as mybir
+from concourse.masks import make_identity
+
+F32 = mybir.dt.float32
+BF16 = mybir.dt.bfloat16
+U32 = mybir.dt.uint32
+U8 = mybir.dt.uint8
+FP8X4 = mybir.dt.float8_e4m3fn_x4
+MULT = mybir.AluOpType.mult
+ADD = mybir.AluOpType.add
+
+P = 128
+PACK = 4
+K_PASS = P * PACK
+BANK = 512
+
+TOKENS = 4 * 256
+HIDDEN = 2048
+RANK = 512
+MODES = 128
+ALPHA = 0.35
+
+TILES = TOKENS // P
+PASSES = HIDDEN // K_PASS
+PIECES = HIDDEN // BANK
+
+FLOPS = 2 * TOKENS * HIDDEN * RANK * 2 + 2 * TOKENS * MODES * RANK
+
+
+def tile_persistentcontrollayer_pb_kernel(tc, hidden_states, Wd, Wu, mode_probs, gate, out):
+    nc = tc.nc
+
+    x_dram = hidden_states.flatten_outer_dims().rearrange("(p i) h -> p (i h)", i=TILES)
+    out_dram = out.flatten_outer_dims().rearrange("(p i) h -> p i h", i=TILES)
+    probs_dram = mode_probs.flatten_outer_dims().rearrange("(p i) k -> p (i k)", i=TILES)
+    wd_dram = Wd.rearrange("(u p e) h -> p u (e h)", u=2, e=2)
+    wu_dram = Wu.rearrange("(j p e) k -> p j (e k)", p=P, e=2)
+
+    with ExitStack() as ctx:
+        keep = ctx.enter_context(tc.tile_pool(name="keep", bufs=1))
+        work = ctx.enter_context(tc.tile_pool(name="work", bufs=3))
+        psum = ctx.enter_context(tc.psum_pool(name="psum", bufs=1))
+        ctx.enter_context(tc.manual_schedule())
+
+        probs_sb = keep.tile([P, TILES * MODES], BF16)
+        nc.sync.dma_start(out=probs_sb[:], in_=probs_dram)
+        gate_sb = keep.tile([P, RANK], BF16)
+        nc.sync.dma_start(out=gate_sb[:], in_=gate)
+        wd_sb = keep.tile([P, PACK * HIDDEN], BF16)
+        for u in range(2):
+            nc.sync.dma_start(out=wd_sb[:, 2 * u * HIDDEN : (2 * u + 2) * HIDDEN], in_=wd_dram[:, u, :])
+        x_sb = keep.tile([P, TILES * HIDDEN], BF16)
+        wu_sb = keep.tile([P, PIECES * PACK * RANK], BF16)
+
+        def load_tokens(pair):
+            cols = slice(2 * pair * HIDDEN, (2 * pair + 2) * HIDDEN)
+            nc.sync.dma_start(out=x_sb[:, cols], in_=x_dram[:, cols])
+
+        load_tokens(0)
+        for n in range(PIECES):
+            nc.sync.dma_start(
+                out=wu_sb[:, n * PACK * RANK : (n + 1) * PACK * RANK].rearrange("p (j c) -> p j c", j=2),
+                in_=wu_dram[:, 2 * n : 2 * n + 2, :],
+            )
+        for pair in range(1, TILES // 2):
+            load_tokens(pair)
+
+        x_words = x_sb[:].bitcast(F32)
+        wd_words = wd_sb[:].bitcast(F32)
+        wu_words = wu_sb[:].bitcast(F32)
+
+        ident_f32 = keep.tile([P, P], F32)
+        make_identity(nc, ident_f32[:])
+        ident_bf16 = keep.tile([P, P], BF16)
+        make_identity(nc, ident_bf16[:])
+
+        def copy_out(which, dst, src):
+            if which % 2 == 0:
+                nc.scalar.copy(out=dst, in_=src)
+            else:
+                nc.vector.tensor_copy(out=dst, in_=src)
+
+        def transpose_rows(words, grouped, bank_tag, bank_bufs, both_engines):
+            grouped_words = grouped.bitcast(F32).rearrange("p (g r u) -> p g r u", g=PASSES, u=2)
+            for b in range(PASSES // 2):
+                bank = psum.tile([P, 2, 2, P], F32, tag=bank_tag, bufs=bank_bufs)
+                for g2 in range(2):
+                    for u in range(2):
+                        first = (2 * b + g2) * 2 * P + u * P
+                        nc.tensor.transpose(bank[:, g2, u, :], words[:, first : first + P], ident_f32[:])
+                copy_out(
+                    b if both_engines else 0,
+                    grouped_words[:, 2 * b : 2 * b + 2, :, :],
+                    bank[:].rearrange("p g u r -> p g r u"),
+                )
+
+        gate_by_chunk = keep.tile([P, RANK], BF16)
+        nc.vector.tensor_copy(
+            out=gate_by_chunk[:].rearrange("k (u e m) -> k u e m", u=2, e=2),
+            in_=gate_sb[:].rearrange("k (u m e) -> k u e m", u=2, e=2),
+        )
+
+        probs_t_ps = psum.tile([P, TILES * P], BF16, tag="tp", bufs=2)
+        for i in range(TILES):
+            nc.tensor.transpose(probs_t_ps[:, i * P : (i + 1) * P], probs_sb[:, i * MODES : (i + 1) * MODES], ident_bf16[:])
+        probs_t = keep.tile([P, TILES * P], BF16)
+        nc.scalar.copy(out=probs_t[:], in_=probs_t_ps[:])
+
+        wd_grouped = keep.tile([P, PACK * HIDDEN], BF16, align_bytes=64)
+        wd_codes = keep.tile([P, PACK * K_PASS], U32, align_bytes=64)
+        wd_scales = keep.tile([P, PACK * K_PASS], U8, align_bytes=64)
+        for t in range(PACK):
+            transpose_rows(
+                wd_words[:, t * HIDDEN // 2 : (t + 1) * HIDDEN // 2],
+                wd_grouped[:, t * HIDDEN : (t + 1) * HIDDEN],
+                "o", PIECES, True,
+            )
+            nc.vector.quantize_mx(
+                out=wd_codes[:, t * K_PASS : (t + 1) * K_PASS].bitcast(FP8X4),
+                scales=wd_scales[:, t * K_PASS : (t + 1) * K_PASS],
+                in_=wd_grouped[:, t * HIDDEN : (t + 1) * HIDDEN],
+            )
+
+        x_codes = {}
+        x_scales = {}
+        h_grouped = {}
+        h_codes = {}
+        h_scales = {}
+
+        def prepare_tokens(i):
+            grouped = work.tile([P, HIDDEN], BF16, tag="x_grouped", align_bytes=64)
+            transpose_rows(x_words[:, i * HIDDEN // 2 : (i + 1) * HIDDEN // 2], grouped[:], "tp", 2, False)
+            x_codes[i] = work.tile([P, K_PASS], U32, tag="x_codes", name="x_codes", align_bytes=64)
+            x_scales[i] = work.tile([P, K_PASS], U8, tag="x_scales", name="x_scales", align_bytes=64)
+            nc.vector.quantize_mx(out=x_codes[i][:].bitcast(FP8X4), scales=x_scales[i][:], in_=grouped[:])
+
+        def first_stage(i):
+            gate_mix_ps = psum.tile([P, PACK, P], F32, tag="wg", bufs=1)
+            for t in range(PACK):
+                nc.tensor.matmul(
+                    gate_mix_ps[:, t, :],
+                    lhsT=gate_by_chunk[:, t * P : (t + 1) * P],
+                    rhs=probs_t[:, i * P : (i + 1) * P],
+                    start=True,
+                    stop=True,
+                )
+            gate_mix = work.tile([P, P, PACK], F32, tag="gate_mix")
+            nc.scalar.copy(out=gate_mix[:], in_=gate_mix_ps[:].rearrange("p t r -> p r t"))
+            low_rank = psum.tile([P, PACK, P], F32, tag="lr", bufs=1)
+            for t in range(PACK):
+                for g in range(PASSES):
+                    w_cols = slice(t * K_PASS + g * P, t * K_PASS + (g + 1) * P)
+                    x_cols = slice(g * P, (g + 1) * P)
+                    nc.tensor.matmul_mx(
+                        out=low_rank[:, t, :],
+                        lhsT=wd_codes[:, w_cols].bitcast(FP8X4),
+                        lhsT_scale=wd_scales[:, w_cols],
+                        rhs=x_codes[i][:, x_cols].bitcast(FP8X4),
+                        rhs_scale=x_scales[i][:, x_cols],
+                        start=(g == 0),
+                        stop=(g == PASSES - 1),
+                    )
+            h_grouped[i] = work.tile([P, P, PACK], BF16, tag="h_grouped", name="h_grouped", align_bytes=64)
+            nc.vector.tensor_tensor(
+                out=h_grouped[i][:],
+                in0=low_rank[:].rearrange("p t r -> p r t"),
+                in1=gate_mix[:],
+                op=MULT,
+            )
+
+        def quantise_h(i):
+            h_codes[i] = work.tile([P, P], U32, tag="h_codes", name="h_codes", align_bytes=64)
+            h_scales[i] = work.tile([P, P], U8, tag="h_scales", name="h_scales", align_bytes=64)
+            nc.vector.quantize_mx(
+                out=h_codes[i][:].bitcast(FP8X4),
+                scales=h_scales[i][:],
+                in_=h_grouped[i][:].rearrange("p r t -> p (r t)"),
+            )
+
+        wu_grouped = keep.tile([P, PACK * HIDDEN], BF16, align_bytes=64)
+        wu_codes = keep.tile([P, HIDDEN], U32, align_bytes=64)
+        wu_scales = keep.tile([P, HIDDEN], U8, align_bytes=64)
+
+        def prepare_wu(n):
+            grouped = wu_grouped[:, n * PACK * BANK : (n + 1) * PACK * BANK]
+            grouped_words = grouped.bitcast(F32).rearrange("p (j r e u) -> p j r e u", j=2, e=2, u=2)
+            for j2 in range(2):
+                bank = psum.tile([P, 2, 2, P], F32, tag="o", bufs=PIECES)
+                for e in range(2):
+                    for u in range(2):
+                        first = ((2 * n + j2) * 2 + e) * RANK // 2 + u * P
+                        nc.tensor.transpose(bank[:, e, u, :], wu_words[:, first : first + P], ident_f32[:])
+                copy_out(j2, grouped_words[:, j2, :, :, :], bank[:].rearrange("p e u r -> p r e u"))
+            nc.vector.quantize_mx(
+                out=wu_codes[:, n * BANK : (n + 1) * BANK].bitcast(FP8X4),
+                scales=wu_scales[:, n * BANK : (n + 1) * BANK],
+                in_=grouped,
+            )
+
+        results = {}
+
+        def second_stage(i, pieces):
+            for n in pieces:
+                cols = slice(n * BANK, (n + 1) * BANK)
+                delta = psum.tile([P, BANK], F32, tag="o", bufs=PIECES)
+                nc.tensor.matmul_mx(
+                    out=delta[:],
+                    lhsT=h_codes[i][:].bitcast(FP8X4),
+                    lhsT_scale=h_scales[i][:],
+                    rhs=wu_codes[:, cols].bitcast(FP8X4),
+                    rhs_scale=wu_scales[:, cols],
+                    start=True,
+                    stop=True,
+                )
+                nc.vector.scalar_tensor_tensor(
+                    out=results[i][:, cols],
+                    in0=delta[:],
+                    scalar=ALPHA,
+                    in1=x_sb[:, i * HIDDEN + n * BANK : i * HIDDEN + (n + 1) * BANK],
+                    op0=MULT,
+                    op1=ADD,
+                )
+
+        prepare_tokens(0)
+        prepare_tokens(1)
+        first_stage(0)
+        quantise_h(0)
+        for n in range(PIECES):
+            prepare_wu(n)
+
+        for i in range(TILES):
+            if i + 2 < TILES:
+                prepare_tokens(i + 2)
+            if i + 1 < TILES:
+                first_stage(i + 1)
+            results[i] = work.tile([P, HIDDEN], F32, tag="result", name="result")
+            second_stage(i, range(0, 1))
+            if i + 1 < TILES:
+                quantise_h(i + 1)
+            second_stage(i, range(1, PIECES))
+            nc.sync.dma_start(out=out_dram[:, i, :], in_=results[i][:])

@@ -25,6 +25,7 @@ ALPHA = 0.35
 TILES = TOKENS // P
 PASSES = HIDDEN // K_PASS
 PIECES = HIDDEN // BANK
+GPSIMD_PIECES = 1
 
 FLOPS = 2 * TOKENS * HIDDEN * RANK * 2 + 2 * TOKENS * MODES * RANK
 
@@ -33,7 +34,7 @@ def tile_persistentcontrollayer_pb_kernel(tc, hidden_states, Wd, Wu, mode_probs,
     nc = tc.nc
 
     x_dram = hidden_states.flatten_outer_dims().rearrange("(p i) h -> p (i h)", i=TILES)
-    out_dram = out.flatten_outer_dims().rearrange("(p i) h -> p i h", i=TILES)
+    out_dram = out.flatten_outer_dims().rearrange("(p i) h -> p (i h)", i=TILES)
     probs_dram = mode_probs.flatten_outer_dims().rearrange("(p i) k -> p (i k)", i=TILES)
     wd_dram = Wd.rearrange("(u p e) h -> p u (e h)", u=2, e=2)
     wu_dram = Wu.rearrange("(j p e) k -> p j (e k)", p=P, e=2)
@@ -43,6 +44,12 @@ def tile_persistentcontrollayer_pb_kernel(tc, hidden_states, Wd, Wu, mode_probs,
         work = ctx.enter_context(tc.tile_pool(name="work", bufs=3))
         psum = ctx.enter_context(tc.psum_pool(name="psum", bufs=1))
         ctx.enter_context(tc.manual_schedule())
+
+        def transpose_bank():
+            return psum.tile([P, 2, 2, P], F32, tag="tp", name="transpose_bank", bufs=3)
+
+        def wide_bank():
+            return psum.tile([P, 2, 2, P], F32, tag="o", name="wide_bank", bufs=PIECES)
 
         probs_sb = keep.tile([P, TILES * MODES], BF16)
         nc.sync.dma_start(out=probs_sb[:], in_=probs_dram)
@@ -71,10 +78,10 @@ def tile_persistentcontrollayer_pb_kernel(tc, hidden_states, Wd, Wu, mode_probs,
         wd_words = wd_sb[:].bitcast(F32)
         wu_words = wu_sb[:].bitcast(F32)
 
-        ident_f32 = keep.tile([P, P], F32)
-        make_identity(nc, ident_f32[:])
         ident_bf16 = keep.tile([P, P], BF16)
         make_identity(nc, ident_bf16[:])
+        ident_f32 = keep.tile([P, P], F32)
+        make_identity(nc, ident_f32[:])
 
         def copy_out(which, dst, src):
             if which % 2 == 0:
@@ -82,10 +89,10 @@ def tile_persistentcontrollayer_pb_kernel(tc, hidden_states, Wd, Wu, mode_probs,
             else:
                 nc.vector.tensor_copy(out=dst, in_=src)
 
-        def transpose_rows(words, grouped, bank_tag, bank_bufs, both_engines):
+        def transpose_rows(words, grouped, new_bank, both_engines):
             grouped_words = grouped.bitcast(F32).rearrange("p (g r u) -> p g r u", g=PASSES, u=2)
             for b in range(PASSES // 2):
-                bank = psum.tile([P, 2, 2, P], F32, tag=bank_tag, bufs=bank_bufs)
+                bank = new_bank()
                 for g2 in range(2):
                     for u in range(2):
                         first = (2 * b + g2) * 2 * P + u * P
@@ -102,26 +109,48 @@ def tile_persistentcontrollayer_pb_kernel(tc, hidden_states, Wd, Wu, mode_probs,
             in_=gate_sb[:].rearrange("k (u m e) -> k u e m", u=2, e=2),
         )
 
-        probs_t_ps = psum.tile([P, TILES * P], BF16, tag="tp", bufs=2)
-        for i in range(TILES):
-            nc.tensor.transpose(probs_t_ps[:, i * P : (i + 1) * P], probs_sb[:, i * MODES : (i + 1) * MODES], ident_bf16[:])
         probs_t = keep.tile([P, TILES * P], BF16)
-        nc.scalar.copy(out=probs_t[:], in_=probs_t_ps[:])
+        for half in range(2):
+            probs_t_ps = psum.tile([P, TILES // 2 * P], BF16, tag="tp", bufs=3)
+            for a in range(TILES // 2):
+                i = half * TILES // 2 + a
+                nc.tensor.transpose(probs_t_ps[:, a * P : (a + 1) * P], probs_sb[:, i * MODES : (i + 1) * MODES], ident_bf16[:])
+            copy_out(half, probs_t[:, half * TILES // 2 * P : (half + 1) * TILES // 2 * P], probs_t_ps[:])
+
+        gate_mix = keep.tile([P, TILES, P, PACK], F32)
+        for i in range(TILES):
+            gate_mix_ps = psum.tile([P, PACK, P], F32, tag="o", bufs=PIECES)
+            for t in range(PACK):
+                nc.tensor.matmul(
+                    gate_mix_ps[:, t, :],
+                    lhsT=gate_by_chunk[:, t * P : (t + 1) * P],
+                    rhs=probs_t[:, i * P : (i + 1) * P],
+                    start=True,
+                    stop=True,
+                )
+            copy_out(i, gate_mix[:, i, :, :], gate_mix_ps[:].rearrange("p t r -> p r t"))
 
         wd_grouped = keep.tile([P, PACK * HIDDEN], BF16, align_bytes=64)
         wd_codes = keep.tile([P, PACK * K_PASS], U32, align_bytes=64)
         wd_scales = keep.tile([P, PACK * K_PASS], U8, align_bytes=64)
-        for t in range(PACK):
-            transpose_rows(
-                wd_words[:, t * HIDDEN // 2 : (t + 1) * HIDDEN // 2],
-                wd_grouped[:, t * HIDDEN : (t + 1) * HIDDEN],
-                "o", PIECES, True,
-            )
+
+        def quantise_wd(t):
             nc.vector.quantize_mx(
                 out=wd_codes[:, t * K_PASS : (t + 1) * K_PASS].bitcast(FP8X4),
                 scales=wd_scales[:, t * K_PASS : (t + 1) * K_PASS],
                 in_=wd_grouped[:, t * HIDDEN : (t + 1) * HIDDEN],
             )
+
+        for t in range(PACK):
+            transpose_rows(
+                wd_words[:, t * HIDDEN // 2 : (t + 1) * HIDDEN // 2],
+                wd_grouped[:, t * HIDDEN : (t + 1) * HIDDEN],
+                wide_bank,
+                True,
+            )
+            if t > 0:
+                quantise_wd(t - 1)
+        quantise_wd(PACK - 1)
 
         x_codes = {}
         x_scales = {}
@@ -131,23 +160,12 @@ def tile_persistentcontrollayer_pb_kernel(tc, hidden_states, Wd, Wu, mode_probs,
 
         def prepare_tokens(i):
             grouped = work.tile([P, HIDDEN], BF16, tag="x_grouped", align_bytes=64)
-            transpose_rows(x_words[:, i * HIDDEN // 2 : (i + 1) * HIDDEN // 2], grouped[:], "tp", 2, False)
+            transpose_rows(x_words[:, i * HIDDEN // 2 : (i + 1) * HIDDEN // 2], grouped[:], transpose_bank, False)
             x_codes[i] = work.tile([P, K_PASS], U32, tag="x_codes", name="x_codes", align_bytes=64)
             x_scales[i] = work.tile([P, K_PASS], U8, tag="x_scales", name="x_scales", align_bytes=64)
             nc.vector.quantize_mx(out=x_codes[i][:].bitcast(FP8X4), scales=x_scales[i][:], in_=grouped[:])
 
         def first_stage(i):
-            gate_mix_ps = psum.tile([P, PACK, P], F32, tag="wg", bufs=1)
-            for t in range(PACK):
-                nc.tensor.matmul(
-                    gate_mix_ps[:, t, :],
-                    lhsT=gate_by_chunk[:, t * P : (t + 1) * P],
-                    rhs=probs_t[:, i * P : (i + 1) * P],
-                    start=True,
-                    stop=True,
-                )
-            gate_mix = work.tile([P, P, PACK], F32, tag="gate_mix")
-            nc.scalar.copy(out=gate_mix[:], in_=gate_mix_ps[:].rearrange("p t r -> p r t"))
             low_rank = psum.tile([P, PACK, P], F32, tag="lr", bufs=1)
             for t in range(PACK):
                 for g in range(PASSES):
@@ -166,7 +184,7 @@ def tile_persistentcontrollayer_pb_kernel(tc, hidden_states, Wd, Wu, mode_probs,
             nc.vector.tensor_tensor(
                 out=h_grouped[i][:],
                 in0=low_rank[:].rearrange("p t r -> p r t"),
-                in1=gate_mix[:],
+                in1=gate_mix[:, i, :, :],
                 op=MULT,
             )
 
@@ -187,12 +205,12 @@ def tile_persistentcontrollayer_pb_kernel(tc, hidden_states, Wd, Wu, mode_probs,
             grouped = wu_grouped[:, n * PACK * BANK : (n + 1) * PACK * BANK]
             grouped_words = grouped.bitcast(F32).rearrange("p (j r e u) -> p j r e u", j=2, e=2, u=2)
             for j2 in range(2):
-                bank = psum.tile([P, 2, 2, P], F32, tag="o", bufs=PIECES)
+                bank = wide_bank()
                 for e in range(2):
                     for u in range(2):
                         first = ((2 * n + j2) * 2 + e) * RANK // 2 + u * P
                         nc.tensor.transpose(bank[:, e, u, :], wu_words[:, first : first + P], ident_f32[:])
-                copy_out(j2, grouped_words[:, j2, :, :, :], bank[:].rearrange("p e u r -> p r e u"))
+                nc.scalar.copy(out=grouped_words[:, j2, :, :, :], in_=bank[:].rearrange("p e u r -> p r e u"))
             nc.vector.quantize_mx(
                 out=wu_codes[:, n * BANK : (n + 1) * BANK].bitcast(FP8X4),
                 scales=wu_scales[:, n * BANK : (n + 1) * BANK],
@@ -204,6 +222,7 @@ def tile_persistentcontrollayer_pb_kernel(tc, hidden_states, Wd, Wu, mode_probs,
         def second_stage(i, pieces):
             for n in pieces:
                 cols = slice(n * BANK, (n + 1) * BANK)
+                residual = x_sb[:, i * HIDDEN + n * BANK : i * HIDDEN + (n + 1) * BANK]
                 delta = psum.tile([P, BANK], F32, tag="o", bufs=PIECES)
                 nc.tensor.matmul_mx(
                     out=delta[:],
@@ -214,21 +233,22 @@ def tile_persistentcontrollayer_pb_kernel(tc, hidden_states, Wd, Wu, mode_probs,
                     start=True,
                     stop=True,
                 )
-                nc.vector.scalar_tensor_tensor(
-                    out=results[i][:, cols],
-                    in0=delta[:],
-                    scalar=ALPHA,
-                    in1=x_sb[:, i * HIDDEN + n * BANK : i * HIDDEN + (n + 1) * BANK],
-                    op0=MULT,
-                    op1=ADD,
-                )
+                if n < GPSIMD_PIECES:
+                    nc.scalar.mul(out=results[i][:, cols], in_=delta[:], mul=ALPHA)
+                    nc.gpsimd.tensor_tensor(out=results[i][:, cols], in0=results[i][:, cols], in1=residual, op=ADD)
+                else:
+                    nc.vector.scalar_tensor_tensor(
+                        out=results[i][:, cols], in0=delta[:], scalar=ALPHA, in1=residual, op0=MULT, op1=ADD
+                    )
 
         prepare_tokens(0)
         prepare_tokens(1)
+        prepare_wu(0)
+        prepare_wu(1)
         first_stage(0)
         quantise_h(0)
-        for n in range(PIECES):
-            prepare_wu(n)
+        prepare_wu(2)
+        prepare_wu(3)
 
         for i in range(TILES):
             if i + 2 < TILES:
@@ -236,8 +256,12 @@ def tile_persistentcontrollayer_pb_kernel(tc, hidden_states, Wd, Wu, mode_probs,
             if i + 1 < TILES:
                 first_stage(i + 1)
             results[i] = work.tile([P, HIDDEN], F32, tag="result", name="result")
-            second_stage(i, range(0, 1))
+            second_stage(i, range(0, GPSIMD_PIECES + 1))
             if i + 1 < TILES:
                 quantise_h(i + 1)
-            second_stage(i, range(1, PIECES))
-            nc.sync.dma_start(out=out_dram[:, i, :], in_=results[i][:])
+            second_stage(i, range(GPSIMD_PIECES + 1, PIECES))
+            for n in list(range(GPSIMD_PIECES, PIECES)) + list(range(GPSIMD_PIECES)):
+                nc.sync.dma_start(
+                    out=out_dram[:, i * HIDDEN + n * BANK : i * HIDDEN + (n + 1) * BANK],
+                    in_=results[i][:, n * BANK : (n + 1) * BANK],
+                )

@@ -25,7 +25,7 @@ ALPHA = 0.35
 TILES = TOKENS // P
 PASSES = HIDDEN // K_PASS
 PIECES = HIDDEN // BANK
-GPSIMD_PIECES = 1
+GPSIMD_PIECES = 2
 
 FLOPS = 2 * TOKENS * HIDDEN * RANK * 2 + 2 * TOKENS * MODES * RANK
 

@@ -25,7 +25,7 @@ ALPHA = 0.35
 TILES = TOKENS // P
 PASSES = HIDDEN // K_PASS
 PIECES = HIDDEN // BANK
-GPSIMD_PIECES = 2
+GPSIMD_PIECES = 0
 
 FLOPS = 2 * TOKENS * HIDDEN * RANK * 2 + 2 * TOKENS * MODES * RANK
 

@@ -25,7 +25,7 @@ ALPHA = 0.35
 TILES = TOKENS // P
 PASSES = HIDDEN // K_PASS
 PIECES = HIDDEN // BANK
-GPSIMD_PIECES = 0
+G_COLS = 512
 
 FLOPS = 2 * TOKENS * HIDDEN * RANK * 2 + 2 * TOKENS * MODES * RANK
 
@@ -36,43 +36,44 @@ def tile_persistentcontrollayer_pb_kernel(tc, hidden_states, Wd, Wu, mode_probs,
     x_dram = hidden_states.flatten_outer_dims().rearrange("(p i) h -> p (i h)", i=TILES)
     out_dram = out.flatten_outer_dims().rearrange("(p i) h -> p (i h)", i=TILES)
     probs_dram = mode_probs.flatten_outer_dims().rearrange("(p i) k -> p (i k)", i=TILES)
-    wd_dram = Wd.rearrange("(u p e) h -> p u (e h)", u=2, e=2)
+    wd_dram = Wd.rearrange("(u p e) h -> p u e h", u=2, e=2)
     wu_dram = Wu.rearrange("(j p e) k -> p j (e k)", p=P, e=2)
 
     with ExitStack() as ctx:
         keep = ctx.enter_context(tc.tile_pool(name="keep", bufs=1))
-        work = ctx.enter_context(tc.tile_pool(name="work", bufs=3))
+        work = ctx.enter_context(tc.tile_pool(name="work", bufs=4))
         psum = ctx.enter_context(tc.psum_pool(name="psum", bufs=1))
         ctx.enter_context(tc.manual_schedule())
 
-        def transpose_bank():
-            return psum.tile([P, 2, 2, P], F32, tag="tp", name="transpose_bank", bufs=3)
-
-        def wide_bank():
-            return psum.tile([P, 2, 2, P], F32, tag="o", name="wide_bank", bufs=PIECES)
+        def new_bank(shape, dtype=F32):
+            return psum.tile(shape, dtype, tag="bank", name="bank", bufs=8)
 
         probs_sb = keep.tile([P, TILES * MODES], BF16)
         nc.sync.dma_start(out=probs_sb[:], in_=probs_dram)
         gate_sb = keep.tile([P, RANK], BF16)
         nc.sync.dma_start(out=gate_sb[:], in_=gate)
         wd_sb = keep.tile([P, PACK * HIDDEN], BF16)
-        for u in range(2):
-            nc.sync.dma_start(out=wd_sb[:, 2 * u * HIDDEN : (2 * u + 2) * HIDDEN], in_=wd_dram[:, u, :])
+        for t in range(PACK):
+            nc.sync.dma_start(out=wd_sb[:, t * HIDDEN : (t + 1) * HIDDEN], in_=wd_dram[:, t // 2, t % 2, :])
         x_sb = keep.tile([P, TILES * HIDDEN], BF16)
         wu_sb = keep.tile([P, PIECES * PACK * RANK], BF16)
 
-        def load_tokens(pair):
-            cols = slice(2 * pair * HIDDEN, (2 * pair + 2) * HIDDEN)
+        def load_tokens(first, count):
+            cols = slice(first * HIDDEN, (first + count) * HIDDEN)
             nc.sync.dma_start(out=x_sb[:, cols], in_=x_dram[:, cols])
 
-        load_tokens(0)
-        for n in range(PIECES):
+        def load_wu(n):
             nc.sync.dma_start(
                 out=wu_sb[:, n * PACK * RANK : (n + 1) * PACK * RANK].rearrange("p (j c) -> p j c", j=2),
                 in_=wu_dram[:, 2 * n : 2 * n + 2, :],
             )
-        for pair in range(1, TILES // 2):
-            load_tokens(pair)
+
+        load_tokens(0, 1)
+        load_tokens(1, 1)
+        for n in range(PIECES):
+            load_wu(n)
+        for i in range(2, TILES):
+            load_tokens(i, 1)
 
         x_words = x_sb[:].bitcast(F32)
         wd_words = wd_sb[:].bitcast(F32)
@@ -83,22 +84,22 @@ def tile_persistentcontrollayer_pb_kernel(tc, hidden_states, Wd, Wu, mode_probs,
         ident_f32 = keep.tile([P, P], F32)
         make_identity(nc, ident_f32[:])
 
-        def copy_out(which, dst, src):
-            if which % 2 == 0:
-                nc.scalar.copy(out=dst, in_=src)
-            else:
+        def copy_out(on_vector, dst, src):
+            if on_vector:
                 nc.vector.tensor_copy(out=dst, in_=src)
+            else:
+                nc.scalar.copy(out=dst, in_=src)
 
-        def transpose_rows(words, grouped, new_bank, both_engines):
+        def transpose_rows(words, grouped, on_vector):
             grouped_words = grouped.bitcast(F32).rearrange("p (g r u) -> p g r u", g=PASSES, u=2)
             for b in range(PASSES // 2):
-                bank = new_bank()
+                bank = new_bank([P, 2, 2, P])
                 for g2 in range(2):
                     for u in range(2):
                         first = (2 * b + g2) * 2 * P + u * P
                         nc.tensor.transpose(bank[:, g2, u, :], words[:, first : first + P], ident_f32[:])
                 copy_out(
-                    b if both_engines else 0,
+                    on_vector[b],
                     grouped_words[:, 2 * b : 2 * b + 2, :, :],
                     bank[:].rearrange("p g u r -> p g r u"),
                 )
@@ -111,28 +112,43 @@ def tile_persistentcontrollayer_pb_kernel(tc, hidden_states, Wd, Wu, mode_probs,
 
         probs_t = keep.tile([P, TILES * P], BF16)
         for half in range(2):
-            probs_t_ps = psum.tile([P, TILES // 2 * P], BF16, tag="tp", bufs=3)
+            probs_t_ps = new_bank([P, TILES // 2 * P], BF16)
             for a in range(TILES // 2):
                 i = half * TILES // 2 + a
                 nc.tensor.transpose(probs_t_ps[:, a * P : (a + 1) * P], probs_sb[:, i * MODES : (i + 1) * MODES], ident_bf16[:])
-            copy_out(half, probs_t[:, half * TILES // 2 * P : (half + 1) * TILES // 2 * P], probs_t_ps[:])
+            copy_out(half == 1, probs_t[:, half * TILES // 2 * P : (half + 1) * TILES // 2 * P], probs_t_ps[:])
 
-        gate_mix = keep.tile([P, TILES, P, PACK], F32)
-        for i in range(TILES):
-            gate_mix_ps = psum.tile([P, PACK, P], F32, tag="o", bufs=PIECES)
+        gate_mix = {}
+        x_grouped = {}
+        x_codes = {}
+        x_scales = {}
+        h_grouped = {}
+        h_codes = {}
+        h_scales = {}
+
+        def mix_gate(i, on_vector=False):
+            gate_mix[i] = work.tile([P, P, PACK], F32, tag="gate_mix", name="gate_mix", bufs=8)
+            bank = new_bank([P, PACK, P])
             for t in range(PACK):
                 nc.tensor.matmul(
-                    gate_mix_ps[:, t, :],
+                    bank[:, t, :],
                     lhsT=gate_by_chunk[:, t * P : (t + 1) * P],
                     rhs=probs_t[:, i * P : (i + 1) * P],
                     start=True,
                     stop=True,
                 )
-            copy_out(i, gate_mix[:, i, :, :], gate_mix_ps[:].rearrange("p t r -> p r t"))
+            copy_out(on_vector, gate_mix[i][:], bank[:].rearrange("p t r -> p r t"))
 
         wd_grouped = keep.tile([P, PACK * HIDDEN], BF16, align_bytes=64)
         wd_codes = keep.tile([P, PACK * K_PASS], U32, align_bytes=64)
         wd_scales = keep.tile([P, PACK * K_PASS], U8, align_bytes=64)
+
+        def flip_wd(t, on_vector):
+            transpose_rows(
+                wd_words[:, t * HIDDEN // 2 : (t + 1) * HIDDEN // 2],
+                wd_grouped[:, t * HIDDEN : (t + 1) * HIDDEN],
+                on_vector,
+            )
 
         def quantise_wd(t):
             nc.vector.quantize_mx(
@@ -141,33 +157,22 @@ def tile_persistentcontrollayer_pb_kernel(tc, hidden_states, Wd, Wu, mode_probs,
                 in_=wd_grouped[:, t * HIDDEN : (t + 1) * HIDDEN],
             )
 
-        for t in range(PACK):
-            transpose_rows(
-                wd_words[:, t * HIDDEN // 2 : (t + 1) * HIDDEN // 2],
-                wd_grouped[:, t * HIDDEN : (t + 1) * HIDDEN],
-                wide_bank,
-                True,
-            )
-            if t > 0:
-                quantise_wd(t - 1)
-        quantise_wd(PACK - 1)
+        def flip_tokens(i, on_vector=(False, False)):
+            x_grouped[i] = work.tile([P, HIDDEN], BF16, tag="x_grouped", name="x_grouped", bufs=4, align_bytes=64)
+            transpose_rows(x_words[:, i * HIDDEN // 2 : (i + 1) * HIDDEN // 2], x_grouped[i][:], on_vector)
 
-        x_codes = {}
-        x_scales = {}
-        h_grouped = {}
-        h_codes = {}
-        h_scales = {}
+        def quantise_tokens(i):
+            x_codes[i] = work.tile([P, K_PASS], U32, tag="x_codes", name="x_codes", bufs=8, align_bytes=64)
+            x_scales[i] = work.tile([P, K_PASS], U8, tag="x_scales", name="x_scales", bufs=8, align_bytes=64)
+            nc.vector.quantize_mx(out=x_codes[i][:].bitcast(FP8X4), scales=x_scales[i][:], in_=x_grouped[i][:])
 
-        def prepare_tokens(i):
-            grouped = work.tile([P, HIDDEN], BF16, tag="x_grouped", align_bytes=64)
-            transpose_rows(x_words[:, i * HIDDEN // 2 : (i + 1) * HIDDEN // 2], grouped[:], transpose_bank, False)
-            x_codes[i] = work.tile([P, K_PASS], U32, tag="x_codes", name="x_codes", align_bytes=64)
-            x_scales[i] = work.tile([P, K_PASS], U8, tag="x_scales", name="x_scales", align_bytes=64)
-            nc.vector.quantize_mx(out=x_codes[i][:].bitcast(FP8X4), scales=x_scales[i][:], in_=grouped[:])
+        low_ranks = {}
 
-        def first_stage(i):
-            low_rank = psum.tile([P, PACK, P], F32, tag="lr", bufs=1)
-            for t in range(PACK):
+        def contract(i, chunks):
+            if i not in low_ranks:
+                low_ranks[i] = new_bank([P, PACK, P])
+            low_rank = low_ranks[i]
+            for t in chunks:
                 for g in range(PASSES):
                     w_cols = slice(t * K_PASS + g * P, t * K_PASS + (g + 1) * P)
                     x_cols = slice(g * P, (g + 1) * P)
@@ -180,17 +185,24 @@ def tile_persistentcontrollayer_pb_kernel(tc, hidden_states, Wd, Wu, mode_probs,
                         start=(g == 0),
                         stop=(g == PASSES - 1),
                     )
+
+        def multiply_gate(i):
+            low_rank = low_ranks[i]
             h_grouped[i] = work.tile([P, P, PACK], BF16, tag="h_grouped", name="h_grouped", align_bytes=64)
             nc.vector.tensor_tensor(
                 out=h_grouped[i][:],
                 in0=low_rank[:].rearrange("p t r -> p r t"),
-                in1=gate_mix[:, i, :, :],
+                in1=gate_mix[i][:],
                 op=MULT,
             )
 
+        def first_stage(i):
+            contract(i, range(PACK))
+            multiply_gate(i)
+
         def quantise_h(i):
-            h_codes[i] = work.tile([P, P], U32, tag="h_codes", name="h_codes", align_bytes=64)
-            h_scales[i] = work.tile([P, P], U8, tag="h_scales", name="h_scales", align_bytes=64)
+            h_codes[i] = work.tile([P, P], U32, tag="h_codes", name="h_codes", bufs=8, align_bytes=64)
+            h_scales[i] = work.tile([P, P], U8, tag="h_scales", name="h_scales", bufs=8, align_bytes=64)
             nc.vector.quantize_mx(
                 out=h_codes[i][:].bitcast(FP8X4),
                 scales=h_scales[i][:],
@@ -201,29 +213,29 @@ def tile_persistentcontrollayer_pb_kernel(tc, hidden_states, Wd, Wu, mode_probs,
         wu_codes = keep.tile([P, HIDDEN], U32, align_bytes=64)
         wu_scales = keep.tile([P, HIDDEN], U8, align_bytes=64)
 
-        def prepare_wu(n):
+        def flip_wu(n, on_vector=(False, False)):
             grouped = wu_grouped[:, n * PACK * BANK : (n + 1) * PACK * BANK]
             grouped_words = grouped.bitcast(F32).rearrange("p (j r e u) -> p j r e u", j=2, e=2, u=2)
             for j2 in range(2):
-                bank = wide_bank()
+                bank = new_bank([P, 2, 2, P])
                 for e in range(2):
                     for u in range(2):
                         first = ((2 * n + j2) * 2 + e) * RANK // 2 + u * P
                         nc.tensor.transpose(bank[:, e, u, :], wu_words[:, first : first + P], ident_f32[:])
-                nc.scalar.copy(out=grouped_words[:, j2, :, :, :], in_=bank[:].rearrange("p e u r -> p r e u"))
+                copy_out(on_vector[j2], grouped_words[:, j2, :, :, :], bank[:].rearrange("p e u r -> p r e u"))
+
+        def quantise_wu(n):
             nc.vector.quantize_mx(
                 out=wu_codes[:, n * BANK : (n + 1) * BANK].bitcast(FP8X4),
                 scales=wu_scales[:, n * BANK : (n + 1) * BANK],
-                in_=grouped,
+                in_=wu_grouped[:, n * PACK * BANK : (n + 1) * PACK * BANK],
             )
 
-        results = {}
-
-        def second_stage(i, pieces):
+        def second_stage(i, pieces, on_gpsimd=()):
             for n in pieces:
                 cols = slice(n * BANK, (n + 1) * BANK)
-                residual = x_sb[:, i * HIDDEN + n * BANK : i * HIDDEN + (n + 1) * BANK]
-                delta = psum.tile([P, BANK], F32, tag="o", bufs=PIECES)
+                span = slice(i * HIDDEN + n * BANK, i * HIDDEN + (n + 1) * BANK)
+                delta = new_bank([P, BANK])
                 nc.tensor.matmul_mx(
                     out=delta[:],
                     lhsT=h_codes[i][:].bitcast(FP8X4),
@@ -233,35 +245,69 @@ def tile_persistentcontrollayer_pb_kernel(tc, hidden_states, Wd, Wu, mode_probs,
                     start=True,
                     stop=True,
                 )
-                if n < GPSIMD_PIECES:
-                    nc.scalar.mul(out=results[i][:, cols], in_=delta[:], mul=ALPHA)
-                    nc.gpsimd.tensor_tensor(out=results[i][:, cols], in0=results[i][:, cols], in1=residual, op=ADD)
+                result = work.tile([P, BANK], F32, tag="result", name="result", bufs=12)
+                if n in on_gpsimd:
+                    nc.scalar.mul(out=result[:], in_=delta[:], mul=ALPHA)
+                    for c in range(0, BANK, G_COLS):
+                        part = slice(c, c + G_COLS)
+                        nc.gpsimd.tensor_tensor(
+                            out=result[:, part], in0=result[:, part], in1=x_sb[:, span][:, part], op=ADD
+                        )
                 else:
                     nc.vector.scalar_tensor_tensor(
-                        out=results[i][:, cols], in0=delta[:], scalar=ALPHA, in1=residual, op0=MULT, op1=ADD
+                        out=result[:], in0=delta[:], scalar=ALPHA, in1=x_sb[:, span], op0=MULT, op1=ADD
                     )
+                nc.sync.dma_start(out=out_dram[:, span], in_=result[:])
 
-        prepare_tokens(0)
-        prepare_tokens(1)
-        prepare_wu(0)
-        prepare_wu(1)
-        first_stage(0)
+
+        VS = (True, False)
+        NO = (False, False)
+        mix_gate(0)
+        for t in range(PACK):
+            flip_wd(t, (t % 2 == 0, False))
+            if 1 + t < 2:
+                mix_gate(1 + t)
+            if t > 0:
+                quantise_wd(t - 1)
+        flip_tokens(0, NO)
+        quantise_wd(PACK - 1)
+        flip_tokens(1, NO)
+        quantise_tokens(0)
+        flip_wu(0, NO)
+        quantise_tokens(1)
+        contract(0, (0, 1))
+        flip_wu(1, NO)
+        quantise_wu(0)
+        contract(0, (2, 3))
+        flip_wu(2, NO)
+        multiply_gate(0)
+        quantise_wu(1)
+        contract(1, (0, 1))
+        flip_wu(3, NO)
         quantise_h(0)
-        prepare_wu(2)
-        prepare_wu(3)
-
-        for i in range(TILES):
-            if i + 2 < TILES:
-                prepare_tokens(i + 2)
-            if i + 1 < TILES:
-                first_stage(i + 1)
-            results[i] = work.tile([P, HIDDEN], F32, tag="result", name="result")
-            second_stage(i, range(0, GPSIMD_PIECES + 1))
-            if i + 1 < TILES:
-                quantise_h(i + 1)
-            second_stage(i, range(GPSIMD_PIECES + 1, PIECES))
-            for n in list(range(GPSIMD_PIECES, PIECES)) + list(range(GPSIMD_PIECES)):
-                nc.sync.dma_start(
-                    out=out_dram[:, i * HIDDEN + n * BANK : i * HIDDEN + (n + 1) * BANK],
-                    in_=results[i][:, n * BANK : (n + 1) * BANK],
-                )
+        quantise_wu(2)
+        contract(1, (2, 3))
+        multiply_gate(1)
+        quantise_wu(3)
+        order = [(i, n) for i in range(TILES) for n in range(PIECES)]
+        stage2 = [0]
+        def more(count):
+            for i, n in order[stage2[0] : stage2[0] + count]:
+                second_stage(i, (n,), (n,) if i >= 9 and n in (0,2) else ())
+            stage2[0] += count
+        for i in range(2, TILES + 1):
+            if i < TILES:
+                flip_tokens(i, NO)
+            more(1)
+            if i > 2:
+                contract(i - 1, range(PACK))
+            if i < TILES:
+                quantise_tokens(i)
+            if i > 2:
+                multiply_gate(i - 1)
+            more(1)
+            quantise_h(i - 1)
+            if 2 <= i < TILES:
+                mix_gate(i)
+            more(3-1)
+        more(40)

@@ -158,12 +158,12 @@ def tile_persistentcontrollayer_pb_kernel(tc, hidden_states, Wd, Wu, mode_probs,
             )
 
         def flip_tokens(i, on_vector=(False, False)):
-            x_grouped[i] = work.tile([P, HIDDEN], BF16, tag="x_grouped", name="x_grouped", bufs=4, align_bytes=64)
+            x_grouped[i] = work.tile([P, HIDDEN], BF16, tag="x_grouped", name="x_grouped", bufs=3, align_bytes=64)
             transpose_rows(x_words[:, i * HIDDEN // 2 : (i + 1) * HIDDEN // 2], x_grouped[i][:], on_vector)
 
         def quantise_tokens(i):
-            x_codes[i] = work.tile([P, K_PASS], U32, tag="x_codes", name="x_codes", bufs=8, align_bytes=64)
-            x_scales[i] = work.tile([P, K_PASS], U8, tag="x_scales", name="x_scales", bufs=8, align_bytes=64)
+            x_codes[i] = work.tile([P, K_PASS], U32, tag="x_codes", name="x_codes", bufs=4, align_bytes=64)
+            x_scales[i] = work.tile([P, K_PASS], U8, tag="x_scales", name="x_scales", bufs=4, align_bytes=64)
             nc.vector.quantize_mx(out=x_codes[i][:].bitcast(FP8X4), scales=x_scales[i][:], in_=x_grouped[i][:])
 
         low_ranks = {}
@@ -245,7 +245,7 @@ def tile_persistentcontrollayer_pb_kernel(tc, hidden_states, Wd, Wu, mode_probs,
                     start=True,
                     stop=True,
                 )
-                result = work.tile([P, BANK], F32, tag="result", name="result", bufs=12)
+                result = work.tile([P, BANK], F32, tag="result", name="result", bufs=TILES * PIECES)
                 if n in on_gpsimd:
                     nc.scalar.mul(out=result[:], in_=delta[:], mul=ALPHA)
                     for c in range(0, BANK, G_COLS):

@@ -262,18 +262,21 @@ def tile_persistentcontrollayer_pb_kernel(tc, hidden_states, Wd, Wu, mode_probs,
 
         VS = (True, False)
         NO = (False, False)
-        mix_gate(0)
+        for i in range(3):
+            mix_gate(i, i % 2 == 1)
         for t in range(PACK):
-            flip_wd(t, (t % 2 == 0, False))
-            if 1 + t < 2:
-                mix_gate(1 + t)
+            flip_wd(t, VS)
+            if 3 + t < TILES:
+                mix_gate(3 + t, False)
             if t > 0:
                 quantise_wd(t - 1)
-        flip_tokens(0, NO)
+        flip_tokens(0, VS)
         quantise_wd(PACK - 1)
         flip_tokens(1, NO)
         quantise_tokens(0)
         flip_wu(0, NO)
+        for i in range(3 + PACK, TILES):
+            mix_gate(i, False)
         quantise_tokens(1)
         contract(0, (0, 1))
         flip_wu(1, NO)
@@ -287,27 +290,27 @@ def tile_persistentcontrollayer_pb_kernel(tc, hidden_states, Wd, Wu, mode_probs,
         quantise_h(0)
         quantise_wu(2)
         contract(1, (2, 3))
-        multiply_gate(1)
         quantise_wu(3)
-        order = [(i, n) for i in range(TILES) for n in range(PIECES)]
-        stage2 = [0]
-        def more(count):
-            for i, n in order[stage2[0] : stage2[0] + count]:
-                second_stage(i, (n,), (n,) if i >= 9 and n in (0,2) else ())
-            stage2[0] += count
-        for i in range(2, TILES + 1):
-            if i < TILES:
-                flip_tokens(i, NO)
-            more(1)
-            if i > 2:
-                contract(i - 1, range(PACK))
-            if i < TILES:
-                quantise_tokens(i)
-            if i > 2:
-                multiply_gate(i - 1)
-            more(1)
-            quantise_h(i - 1)
-            if 2 <= i < TILES:
-                mix_gate(i)
-            more(3-1)
-        more(40)
+
+        def gp(i):
+            return (3,)
+        for i in range(0, TILES, 2):
+            if i + 2 < TILES:
+                flip_tokens(i + 2, NO)
+                flip_tokens(i + 3, NO)
+            multiply_gate(i + 1)
+            second_stage(i, (0,), gp(i))
+            quantise_h(i + 1)
+            if i + 2 < TILES:
+                quantise_tokens(i + 2)
+            second_stage(i, (1, 2, 3), gp(i))
+            if i + 2 < TILES:
+                contract(i + 2, range(PACK))
+                quantise_tokens(i + 3)
+                multiply_gate(i + 2)
+            second_stage(i + 1, (0,), gp(i + 1))
+            if i + 2 < TILES:
+                quantise_h(i + 2)
+            second_stage(i + 1, (1, 2, 3), gp(i + 1))
+            if i + 2 < TILES:
+                contract(i + 3, range(PACK))

@@ -72,8 +72,8 @@ def tile_persistentcontrollayer_pb_kernel(tc, hidden_states, Wd, Wu, mode_probs,
         load_tokens(1, 1)
         for n in range(PIECES):
             load_wu(n)
-        for i in range(2, TILES):
-            load_tokens(i, 1)
+        for i in range(2, TILES, 2):
+            load_tokens(i, 2)
 
         x_words = x_sb[:].bitcast(F32)
         wd_words = wd_sb[:].bitcast(F32)
@@ -231,6 +231,8 @@ def tile_persistentcontrollayer_pb_kernel(tc, hidden_states, Wd, Wu, mode_probs,
                 in_=wu_grouped[:, n * PACK * BANK : (n + 1) * PACK * BANK],
             )
 
+        results = {}
+
         def second_stage(i, pieces, on_gpsimd=()):
             for n in pieces:
                 cols = slice(n * BANK, (n + 1) * BANK)
@@ -245,9 +247,11 @@ def tile_persistentcontrollayer_pb_kernel(tc, hidden_states, Wd, Wu, mode_probs,
                     start=True,
                     stop=True,
                 )
-                result = work.tile([P, BANK], F32, tag="result", name="result", bufs=TILES * PIECES)
+                if n % 2 == 0:
+                    results[i] = work.tile([P, 2 * BANK], F32, tag="result", name="result", bufs=TILES * PIECES // 2)
+                result = results[i][:, n % 2 * BANK : (n % 2 + 1) * BANK]
                 if n in on_gpsimd:
-                    nc.scalar.mul(out=result[:], in_=delta[:], mul=ALPHA)
+                    nc.scalar.mul(out=result, in_=delta[:], mul=ALPHA)
                     for c in range(0, BANK, G_COLS):
                         part = slice(c, c + G_COLS)
                         nc.gpsimd.tensor_tensor(
@@ -255,9 +259,11 @@ def tile_persistentcontrollayer_pb_kernel(tc, hidden_states, Wd, Wu, mode_probs,
                         )
                 else:
                     nc.vector.scalar_tensor_tensor(
-                        out=result[:], in0=delta[:], scalar=ALPHA, in1=x_sb[:, span], op0=MULT, op1=ADD
+                        out=result, in0=delta[:], scalar=ALPHA, in1=x_sb[:, span], op0=MULT, op1=ADD
                     )
-                nc.sync.dma_start(out=out_dram[:, span], in_=result[:])
+                if n % 2 == 2 - 1:
+                    store = slice(span.stop - 2 * BANK, span.stop)
+                    nc.sync.dma_start(out=out_dram[:, store], in_=results[i][:])
 
 
         VS = (True, False)

@@ -90,10 +90,22 @@ def tile_persistentcontrollayer_pb_kernel(tc, hidden_states, Wd, Wu, mode_probs,
             else:
                 nc.scalar.copy(out=dst, in_=src)
 
-        def transpose_rows(words, grouped, on_vector):
+        filler = keep.tile([P, BANK], BF16)
+        nc.vector.memset(filler[:], 0.0)
+
+        def keep_busy(bank, columns):
+            nc.tensor.matmul(bank[:, 0:columns], lhsT=filler[:, 0:P], rhs=filler[:, 0:columns], start=True, stop=True)
+
+        first_bank = new_bank([P, BANK])
+        for again in range(6):
+            keep_busy(first_bank[:], BANK)
+
+        def transpose_rows(words, grouped, on_vector, busy_columns=0):
             grouped_words = grouped.bitcast(F32).rearrange("p (g r u) -> p g r u", g=PASSES, u=2)
             for b in range(PASSES // 2):
                 bank = new_bank([P, 2, 2, P])
+                if busy_columns:
+                    keep_busy(bank[:].rearrange("p g u r -> p (g u r)"), busy_columns)
                 for g2 in range(2):
                     for u in range(2):
                         first = (2 * b + g2) * 2 * P + u * P
@@ -112,6 +124,7 @@ def tile_persistentcontrollayer_pb_kernel(tc, hidden_states, Wd, Wu, mode_probs,
 
         probs_t = keep.tile([P, TILES * P], BF16)
         for half in range(2):
+            keep_busy(first_bank[:], BANK)
             probs_t_ps = new_bank([P, TILES // 2 * P], BF16)
             for a in range(TILES // 2):
                 i = half * TILES // 2 + a
@@ -157,9 +170,9 @@ def tile_persistentcontrollayer_pb_kernel(tc, hidden_states, Wd, Wu, mode_probs,
                 in_=wd_grouped[:, t * HIDDEN : (t + 1) * HIDDEN],
             )
 
-        def flip_tokens(i, on_vector=(False, False)):
+        def flip_tokens(i, on_vector=(False, False), busy_columns=0):
             x_grouped[i] = work.tile([P, HIDDEN], BF16, tag="x_grouped", name="x_grouped", bufs=3, align_bytes=64)
-            transpose_rows(x_words[:, i * HIDDEN // 2 : (i + 1) * HIDDEN // 2], x_grouped[i][:], on_vector)
+            transpose_rows(x_words[:, i * HIDDEN // 2 : (i + 1) * HIDDEN // 2], x_grouped[i][:], on_vector, busy_columns)
 
         def quantise_tokens(i):
             x_codes[i] = work.tile([P, K_PASS], U32, tag="x_codes", name="x_codes", bufs=4, align_bytes=64)
@@ -268,21 +281,17 @@ def tile_persistentcontrollayer_pb_kernel(tc, hidden_states, Wd, Wu, mode_probs,
 
         VS = (True, False)
         NO = (False, False)
-        for i in range(3):
-            mix_gate(i, i % 2 == 1)
         for t in range(PACK):
+            mix_gate(2 * t)
+            mix_gate(2 * t + 1, t % 2 == 0)
             flip_wd(t, VS)
-            if 3 + t < TILES:
-                mix_gate(3 + t, False)
             if t > 0:
                 quantise_wd(t - 1)
-        flip_tokens(0, VS)
+        flip_tokens(0, VS, 384)
         quantise_wd(PACK - 1)
-        flip_tokens(1, NO)
+        flip_tokens(1, NO, 384)
         quantise_tokens(0)
         flip_wu(0, NO)
-        for i in range(3 + PACK, TILES):
-            mix_gate(i, False)
         quantise_tokens(1)
         contract(0, (0, 1))
         flip_wu(1, NO)

from contextlib import ExitStack

import concourse.mybir as mybir
from concourse.masks import make_identity

F32 = mybir.dt.float32
BF16 = mybir.dt.bfloat16
U32 = mybir.dt.uint32
U8 = mybir.dt.uint8
FP8X4 = mybir.dt.float8_e4m3fn_x4
MULT = mybir.AluOpType.mult
ADD = mybir.AluOpType.add

P = 128
PACK = 4
K_PASS = P * PACK
BANK = 512

TOKENS = 4 * 256
HIDDEN = 2048
RANK = 512
MODES = 128
ALPHA = 0.35

TILES = TOKENS // P
PASSES = HIDDEN // K_PASS
PIECES = HIDDEN // BANK
G_COLS = 512

FLOPS = 2 * TOKENS * HIDDEN * RANK * 2 + 2 * TOKENS * MODES * RANK


def tile_persistentcontrollayer_pb_kernel(tc, hidden_states, Wd, Wu, mode_probs, gate, out):
    nc = tc.nc

    x_dram = hidden_states.flatten_outer_dims().rearrange("(p i) h -> p (i h)", i=TILES)
    out_dram = out.flatten_outer_dims().rearrange("(p i) h -> p (i h)", i=TILES)
    probs_dram = mode_probs.flatten_outer_dims().rearrange("(p i) k -> p (i k)", i=TILES)
    wd_dram = Wd.rearrange("(u p e) h -> p u e h", u=2, e=2)
    wu_dram = Wu.rearrange("(j p e) k -> p j (e k)", p=P, e=2)

    with ExitStack() as ctx:
        keep = ctx.enter_context(tc.tile_pool(name="keep", bufs=1))
        work = ctx.enter_context(tc.tile_pool(name="work", bufs=4))
        psum = ctx.enter_context(tc.psum_pool(name="psum", bufs=1))
        ctx.enter_context(tc.manual_schedule())

        def new_bank(shape, dtype=F32):
            return psum.tile(shape, dtype, tag="bank", name="bank", bufs=8)

        probs_sb = keep.tile([P, TILES * MODES], BF16)
        nc.sync.dma_start(out=probs_sb[:], in_=probs_dram)
        gate_sb = keep.tile([P, RANK], BF16)
        nc.sync.dma_start(out=gate_sb[:], in_=gate)
        wd_sb = keep.tile([P, PACK * HIDDEN], BF16)
        for t in range(PACK):
            nc.sync.dma_start(out=wd_sb[:, t * HIDDEN : (t + 1) * HIDDEN], in_=wd_dram[:, t // 2, t % 2, :])
        x_sb = keep.tile([P, TILES * HIDDEN], BF16)
        wu_sb = keep.tile([P, PIECES * PACK * RANK], BF16)

        def load_tokens(first, count):
            cols = slice(first * HIDDEN, (first + count) * HIDDEN)
            nc.sync.dma_start(out=x_sb[:, cols], in_=x_dram[:, cols])

        def load_wu(n):
            nc.sync.dma_start(
                out=wu_sb[:, n * PACK * RANK : (n + 1) * PACK * RANK].rearrange("p (j c) -> p j c", j=2),
                in_=wu_dram[:, 2 * n : 2 * n + 2, :],
            )

        load_tokens(0, 1)
        load_tokens(1, 1)
        for n in range(PIECES):
            load_wu(n)
        for i in range(2, TILES, 2):
            load_tokens(i, 2)

        x_words = x_sb[:].bitcast(F32)
        wd_words = wd_sb[:].bitcast(F32)
        wu_words = wu_sb[:].bitcast(F32)

        ident_bf16 = keep.tile([P, P], BF16)
        make_identity(nc, ident_bf16[:])
        ident_f32 = keep.tile([P, P], F32)
        make_identity(nc, ident_f32[:])

        def copy_out(on_vector, dst, src):
            if on_vector:
                nc.vector.tensor_copy(out=dst, in_=src)
            else:
                nc.scalar.copy(out=dst, in_=src)

        filler = keep.tile([P, BANK], BF16)
        nc.vector.memset(filler[:], 0.0)

        def keep_busy(bank, columns):
            nc.tensor.matmul(bank[:, 0:columns], lhsT=filler[:, 0:P], rhs=filler[:, 0:columns], start=True, stop=True)

        first_bank = new_bank([P, BANK])
        for again in range(6):
            keep_busy(first_bank[:], BANK)

        def transpose_rows(words, grouped, on_vector, busy_columns=0):
            grouped_words = grouped.bitcast(F32).rearrange("p (g r u) -> p g r u", g=PASSES, u=2)
            for b in range(PASSES // 2):
                bank = new_bank([P, 2, 2, P])
                if busy_columns:
                    keep_busy(bank[:].rearrange("p g u r -> p (g u r)"), busy_columns)
                for g2 in range(2):
                    for u in range(2):
                        first = (2 * b + g2) * 2 * P + u * P
                        nc.tensor.transpose(bank[:, g2, u, :], words[:, first : first + P], ident_f32[:])
                copy_out(
                    on_vector[b],
                    grouped_words[:, 2 * b : 2 * b + 2, :, :],
                    bank[:].rearrange("p g u r -> p g r u"),
                )

        gate_by_chunk = keep.tile([P, RANK], BF16)
        nc.vector.tensor_copy(
            out=gate_by_chunk[:].rearrange("k (u e m) -> k u e m", u=2, e=2),
            in_=gate_sb[:].rearrange("k (u m e) -> k u e m", u=2, e=2),
        )

        probs_t = keep.tile([P, TILES * P], BF16)
        for half in range(2):
            keep_busy(first_bank[:], BANK)
            probs_t_ps = new_bank([P, TILES // 2 * P], BF16)
            for a in range(TILES // 2):
                i = half * TILES // 2 + a
                nc.tensor.transpose(probs_t_ps[:, a * P : (a + 1) * P], probs_sb[:, i * MODES : (i + 1) * MODES], ident_bf16[:])
            copy_out(half == 1, probs_t[:, half * TILES // 2 * P : (half + 1) * TILES // 2 * P], probs_t_ps[:])

        gate_mix = {}
        x_grouped = {}
        x_codes = {}
        x_scales = {}
        h_grouped = {}
        h_codes = {}
        h_scales = {}

        def mix_gate(i, on_vector=False):
            gate_mix[i] = work.tile([P, P, PACK], F32, tag="gate_mix", name="gate_mix", bufs=8)
            bank = new_bank([P, PACK, P])
            for t in range(PACK):
                nc.tensor.matmul(
                    bank[:, t, :],
                    lhsT=gate_by_chunk[:, t * P : (t + 1) * P],
                    rhs=probs_t[:, i * P : (i + 1) * P],
                    start=True,
                    stop=True,
                )
            copy_out(on_vector, gate_mix[i][:], bank[:].rearrange("p t r -> p r t"))

        wd_grouped = keep.tile([P, PACK * HIDDEN], BF16, align_bytes=64)
        wd_codes = keep.tile([P, PACK * K_PASS], U32, align_bytes=64)
        wd_scales = keep.tile([P, PACK * K_PASS], U8, align_bytes=64)

        def flip_wd(t, on_vector):
            transpose_rows(
                wd_words[:, t * HIDDEN // 2 : (t + 1) * HIDDEN // 2],
                wd_grouped[:, t * HIDDEN : (t + 1) * HIDDEN],
                on_vector,
            )

        def quantise_wd(t):
            nc.vector.quantize_mx(
                out=wd_codes[:, t * K_PASS : (t + 1) * K_PASS].bitcast(FP8X4),
                scales=wd_scales[:, t * K_PASS : (t + 1) * K_PASS],
                in_=wd_grouped[:, t * HIDDEN : (t + 1) * HIDDEN],
            )

        def flip_tokens(i, on_vector=(False, False), busy_columns=0):
            x_grouped[i] = work.tile([P, HIDDEN], BF16, tag="x_grouped", name="x_grouped", bufs=3, align_bytes=64)
            transpose_rows(x_words[:, i * HIDDEN // 2 : (i + 1) * HIDDEN // 2], x_grouped[i][:], on_vector, busy_columns)

        def quantise_tokens(i):
            x_codes[i] = work.tile([P, K_PASS], U32, tag="x_codes", name="x_codes", bufs=4, align_bytes=64)
            x_scales[i] = work.tile([P, K_PASS], U8, tag="x_scales", name="x_scales", bufs=4, align_bytes=64)
            nc.vector.quantize_mx(out=x_codes[i][:].bitcast(FP8X4), scales=x_scales[i][:], in_=x_grouped[i][:])

        low_ranks = {}

        def contract(i, chunks):
            if i not in low_ranks:
                low_ranks[i] = new_bank([P, PACK, P])
            low_rank = low_ranks[i]
            for t in chunks:
                for g in range(PASSES):
                    w_cols = slice(t * K_PASS + g * P, t * K_PASS + (g + 1) * P)
                    x_cols = slice(g * P, (g + 1) * P)
                    nc.tensor.matmul_mx(
                        out=low_rank[:, t, :],
                        lhsT=wd_codes[:, w_cols].bitcast(FP8X4),
                        lhsT_scale=wd_scales[:, w_cols],
                        rhs=x_codes[i][:, x_cols].bitcast(FP8X4),
                        rhs_scale=x_scales[i][:, x_cols],
                        start=(g == 0),
                        stop=(g == PASSES - 1),
                    )

        def multiply_gate(i):
            low_rank = low_ranks[i]
            h_grouped[i] = work.tile([P, P, PACK], BF16, tag="h_grouped", name="h_grouped", align_bytes=64)
            nc.vector.tensor_tensor(
                out=h_grouped[i][:],
                in0=low_rank[:].rearrange("p t r -> p r t"),
                in1=gate_mix[i][:],
                op=MULT,
            )

        def first_stage(i):
            contract(i, range(PACK))
            multiply_gate(i)

        def quantise_h(i):
            h_codes[i] = work.tile([P, P], U32, tag="h_codes", name="h_codes", bufs=8, align_bytes=64)
            h_scales[i] = work.tile([P, P], U8, tag="h_scales", name="h_scales", bufs=8, align_bytes=64)
            nc.vector.quantize_mx(
                out=h_codes[i][:].bitcast(FP8X4),
                scales=h_scales[i][:],
                in_=h_grouped[i][:].rearrange("p r t -> p (r t)"),
            )

        wu_grouped = keep.tile([P, PACK * HIDDEN], BF16, align_bytes=64)
        wu_codes = keep.tile([P, HIDDEN], U32, align_bytes=64)
        wu_scales = keep.tile([P, HIDDEN], U8, align_bytes=64)

        def flip_wu(n, on_vector=(False, False)):
            grouped = wu_grouped[:, n * PACK * BANK : (n + 1) * PACK * BANK]
            grouped_words = grouped.bitcast(F32).rearrange("p (j r e u) -> p j r e u", j=2, e=2, u=2)
            for j2 in range(2):
                bank = new_bank([P, 2, 2, P])
                for e in range(2):
                    for u in range(2):
                        first = ((2 * n + j2) * 2 + e) * RANK // 2 + u * P
                        nc.tensor.transpose(bank[:, e, u, :], wu_words[:, first : first + P], ident_f32[:])
                copy_out(on_vector[j2], grouped_words[:, j2, :, :, :], bank[:].rearrange("p e u r -> p r e u"))

        def quantise_wu(n):
            nc.vector.quantize_mx(
                out=wu_codes[:, n * BANK : (n + 1) * BANK].bitcast(FP8X4),
                scales=wu_scales[:, n * BANK : (n + 1) * BANK],
                in_=wu_grouped[:, n * PACK * BANK : (n + 1) * PACK * BANK],
            )

        results = {}

        def second_stage(i, pieces, on_gpsimd=()):
            for n in pieces:
                cols = slice(n * BANK, (n + 1) * BANK)
                span = slice(i * HIDDEN + n * BANK, i * HIDDEN + (n + 1) * BANK)
                delta = new_bank([P, BANK])
                nc.tensor.matmul_mx(
                    out=delta[:],
                    lhsT=h_codes[i][:].bitcast(FP8X4),
                    lhsT_scale=h_scales[i][:],
                    rhs=wu_codes[:, cols].bitcast(FP8X4),
                    rhs_scale=wu_scales[:, cols],
                    start=True,
                    stop=True,
                )
                if n % 2 == 0:
                    results[i] = work.tile([P, 2 * BANK], F32, tag="result", name="result", bufs=TILES * PIECES // 2)
                result = results[i][:, n % 2 * BANK : (n % 2 + 1) * BANK]
                if n in on_gpsimd:
                    nc.scalar.mul(out=result, in_=delta[:], mul=ALPHA)
                    for c in range(0, BANK, G_COLS):
                        part = slice(c, c + G_COLS)
                        nc.gpsimd.tensor_tensor(
                            out=result[:, part], in0=result[:, part], in1=x_sb[:, span][:, part], op=ADD
                        )
                else:
                    nc.vector.scalar_tensor_tensor(
                        out=result, in0=delta[:], scalar=ALPHA, in1=x_sb[:, span], op0=MULT, op1=ADD
                    )
                if n % 2 == 2 - 1:
                    store = slice(span.stop - 2 * BANK, span.stop)
                    nc.sync.dma_start(out=out_dram[:, store], in_=results[i][:])


        VS = (True, False)
        NO = (False, False)
        for t in range(PACK):
            mix_gate(2 * t)
            mix_gate(2 * t + 1, t % 2 == 0)
            flip_wd(t, VS)
            if t > 0:
                quantise_wd(t - 1)
        flip_tokens(0, VS, 384)
        quantise_wd(PACK - 1)
        flip_tokens(1, NO, 384)
        quantise_tokens(0)
        flip_wu(0, NO)
        quantise_tokens(1)
        contract(0, (0, 1))
        flip_wu(1, NO)
        quantise_wu(0)
        contract(0, (2, 3))
        flip_wu(2, NO)
        multiply_gate(0)
        quantise_wu(1)
        contract(1, (0, 1))
        flip_wu(3, NO)
        quantise_h(0)
        quantise_wu(2)
        contract(1, (2, 3))
        quantise_wu(3)

        def gp(i):
            return (3,)
        for i in range(0, TILES, 2):
            if i + 2 < TILES:
                flip_tokens(i + 2, NO)
                flip_tokens(i + 3, NO)
            multiply_gate(i + 1)
            second_stage(i, (0,), gp(i))
            quantise_h(i + 1)
            if i + 2 < TILES:
                quantise_tokens(i + 2)
            second_stage(i, (1, 2, 3), gp(i))
            if i + 2 < TILES:
                contract(i + 2, range(PACK))
                quantise_tokens(i + 3)
                multiply_gate(i + 2)
            second_stage(i + 1, (0,), gp(i + 1))
            if i + 2 < TILES:
                quantise_h(i + 2)
            second_stage(i + 1, (1, 2, 3), gp(i + 1))
            if i + 2 < TILES:
                contract(i + 3, range(PACK))
